import numpy as np
import ml_dtypes


def mxq(x, axis, fmt="e4m3"):
    dtype, down = {"e4m3": (ml_dtypes.float8_e4m3fn, 7), "e5m2": (ml_dtypes.float8_e5m2, 14)}[fmt]
    v = np.moveaxis(np.asarray(x, np.float32).astype(ml_dtypes.bfloat16).astype(np.float64), axis, -1)
    blocks = v.reshape(v.shape[:-1] + (-1, 32))
    amax = np.abs(blocks).max(-1, keepdims=True)
    byte = np.maximum(np.where(amax > 0, np.frexp(amax)[1] - 1 + 127, 0) - down, 1)
    scale = np.exp2(byte - 127.0)
    codes = (blocks / scale).astype(np.float32).astype(dtype).astype(np.float64)
    return np.moveaxis((codes * scale).reshape(v.shape), -1, axis)


WIDE = False


def mx_kscale(k):
    if not WIDE:
        return np.ones(k)
    levels = np.array([10, -10, 5, -5, 0])
    a = np.random.permutation(np.resize(levels, k // 512 * 4)).reshape(k // 512, 4)
    idx = np.arange(k)
    return np.exp2(a[idx // 512, idx % 128 // 32])


BF16 = ml_dtypes.bfloat16


def bf(x):
    return np.asarray(x, np.float32).astype(BF16)


def f64(x):
    return np.asarray(x).astype(np.float64)


B, N, SIZE, CH = 256, 16, 1024, 512


def sigmoid(v):
    return 1.0 / (1.0 + np.exp(-v))


def setup_inputs():
    s = mx_kscale(SIZE)
    half = np.concatenate([np.ones(CH), np.full(CH, 2.0 / np.sqrt(N))])
    return {"z_node": bf(np.random.standard_normal((B, N, SIZE)) * s),
            "z_children": bf(np.random.standard_normal((B, N, SIZE)) * half),
            "W_f": bf(np.random.standard_normal((CH, SIZE)) / np.sqrt(SIZE) / s),
            "U_f": bf(np.random.standard_normal((CH, CH)) / np.sqrt(CH)),
            "b_f": bf(np.random.standard_normal(CH) * 0.5)}


def reference(z_node, z_children, W_f, U_f, b_f):
    h_k = f64(z_children)[..., :CH]
    c_k = f64(z_children)[..., CH:]
    f_j_k = sigmoid((mxq(f64(z_node), 2, "e4m3") @ mxq(f64(W_f), 1, "e4m3").T) + h_k @ f64(U_f).T + f64(b_f))
    return (f_j_k * c_k).sum(axis=1)

@@ -1,0 +1,330 @@
+from contextlib import ExitStack
+
+import concourse.mybir as mybir
+from concourse.masks import make_identity
+
+F32 = mybir.dt.float32
+BF16 = mybir.dt.bfloat16
+U32 = mybir.dt.uint32
+U8 = mybir.dt.uint8
+FP8X4 = mybir.dt.float8_e4m3fn_x4
+ADD = mybir.AluOpType.add
+MULT = mybir.AluOpType.mult
+SIGMOID = mybir.ActivationFunctionType.Sigmoid
+
+P = 128
+B, N, SIZE, CH = 256, 16, 1024, 512
+FLOPS = 2 * B * N * (SIZE + CH) * CH
+
+NPAIR = 16
+PER_HALF = 8
+ACC_MODE = "pe"
+LAG = 3
+BIAS_PE = ()
+TAIL_FREE = False
+SPLIT_FROM = 15
+
+
+def tile_treelstm_pa_kernel(tc, z_node, z_children, W_f, U_f, b_f, out):
+    nc = tc.nc
+    st = {}
+    with ExitStack() as ctx:
+        const = ctx.enter_context(tc.tile_pool(name="const", bufs=1))
+        data = ctx.enter_context(tc.tile_pool(name="data", bufs=1))
+        work = ctx.enter_context(tc.tile_pool(name="work", bufs=2))
+        psum = ctx.enter_context(tc.psum_pool(name="psum", bufs=1))
+        ctx.enter_context(tc.manual_schedule())
+
+        def bank(tag, bufs):
+            return psum.tile([P, 512], F32, tag=tag, bufs=bufs, name=tag)
+
+        brow = const.tile([P, CH], BF16, name="brow")
+        nc.vector.memset(brow[:], 0.0)
+        nc.scalar.dma_start(out=brow[0:1, :], in_=b_f.rearrange("(o c) -> o c", o=1))
+        ones = const.tile([P, P], BF16, name="ones")
+        nc.vector.memset(ones[:], 1.0)
+        warm = const.tile([P, 8], F32, name="warm")
+        nc.vector.memset(warm[:], 0.0)
+        nc.scalar.activation(out=warm[:], in_=warm[:], func=SIGMOID)
+        ident = const.tile([P, P], F32, name="ident")
+        make_identity(nc, ident[:])
+
+        def load_pair(src, s, nm):
+            bh, j = divmod(s, PER_HALF)
+            t = data.tile([P, 2 * SIZE], BF16, name="%s%d" % (nm, s))
+            nc.sync.dma_start(
+                out=t[:],
+                in_=src[bh * P : (bh + 1) * P, 2 * j : 2 * j + 2, :].rearrange("b n k -> b (n k)"),
+            )
+            return t
+
+        zn = {}
+        zc = {}
+        un = const.tile([P, 4 * CH], BF16, name="un")
+        nc.sync.dma_start(
+            out=un[:].rearrange("p (t k) -> p t k", t=4), in_=U_f.rearrange("(t p) k -> p t k", p=P)
+        )
+        zc[0] = load_pair(z_children, 0, "zc")
+        wn = const.tile([P, 4 * SIZE], BF16, name="wn")
+        nc.sync.dma_start(
+            out=wn[:].rearrange("p (t k) -> p t k", t=4), in_=W_f.rearrange("(t p) k -> p t k", p=P)
+        )
+        zc[1] = load_pair(z_children, 1, "zc")
+        zn[0] = load_pair(z_node, 0, "zn")
+        for s in range(1, NPAIR):
+            if s + 1 < NPAIR:
+                zc[s + 1] = load_pair(z_children, s + 1, "zc")
+            zn[s] = load_pair(z_node, s, "zn")
+
+        def t_h(s, i):
+            if i == 0:
+                st["hps", s] = bank("hps", 1)
+            tl, v = divmod(i, 2)
+            nc.tensor.transpose(
+                st["hps", s][:, i * P : (i + 1) * P],
+                zc[s][:].bitcast(F32)[:, tl * 512 + v * P : tl * 512 + (v + 1) * P],
+                ident[:],
+            )
+
+        def c_h(s):
+            ht = work.tile([P, 512], F32, tag="ht", bufs=2, name="ht")
+            nc.scalar.copy(out=ht[:], in_=st["hps", s][:])
+            st["ht", s] = ht[:].bitcast(BF16).rearrange("p (t v r e) -> p t v r e", t=2, v=2, e=2)
+
+        def t_z(s, i):
+            tl, wb = divmod(i, 4)
+            if wb == 0:
+                st["zps", s, tl] = bank("zps", 2)
+            nc.tensor.transpose(
+                st["zps", s, tl][:, wb * P : (wb + 1) * P],
+                zn[s][:].bitcast(F32)[:, tl * 512 + wb * P : tl * 512 + (wb + 1) * P],
+                ident[:],
+            )
+
+        def c_z(s, tl):
+            if tl == 0:
+                st["zg", s] = work.tile([P, 2048], BF16, tag="zg", bufs=2, name="zg", align_bytes=64)
+            dst = st["zg", s][:].bitcast(F32)[:, tl * 512 : (tl + 1) * 512]
+            nc.scalar.copy(
+                out=dst.rearrange("p (g r u) -> p g r u", g=2, u=2),
+                in_=st["zps", s, tl][:].rearrange("p (g u r) -> p g r u", g=2, u=2),
+            )
+
+        def q_z(s):
+            zq = work.tile([P, 512], U32, tag="zq", bufs=3, name="zq", align_bytes=64)
+            zs = work.tile([P, 512], U8, tag="zs", bufs=3, name="zs", align_bytes=64)
+            nc.vector.quantize_mx(out=zq[:].bitcast(FP8X4), scales=zs[:], in_=st["zg", s][:])
+            st["zq", s] = (zq, zs)
+
+        def bias_on_pe(s, tl):
+            return (2 * s + tl) % 8 in BIAS_PE
+
+        def mm_plain(s, tl, i):
+            if i == 0:
+                st["pl", s, tl] = bank("pl", 2)
+            last = 4 if bias_on_pe(s, tl) else 3
+            if i < 4:
+                v, e = divmod(i, 2)
+                lhs = st["ht", s][:, tl, v, :, e]
+                rhs = ut16[:, v, :, e]
+            else:
+                lhs = ones[:]
+                rhs = brow[:]
+            nc.tensor.matmul(out=st["pl", s, tl][:], lhsT=lhs, rhs=rhs, start=(i == 0), stop=(i == last))
+
+        def mm_mx(s, tl, g):
+            if g == 0:
+                st["mx", s, tl] = bank("mx", 2)
+            zq, zs = st["zq", s]
+            c0 = (tl * 2 + g) * P
+            nc.tensor.matmul_mx(
+                out=st["mx", s, tl][:],
+                lhsT=zq[:, c0 : c0 + P].bitcast(FP8X4),
+                lhsT_scale=zs[:, c0 : c0 + P],
+                rhs=wq[:, g * CH : (g + 1) * CH].bitcast(FP8X4),
+                rhs_scale=ws[:, g * CH : (g + 1) * CH],
+                start=(g == 0),
+                stop=(g == 1),
+            )
+
+        def p1(s, tl):
+            if tl == 0:
+                st["w", s] = work.tile([P, 2 * CH], F32, tag="w", bufs=LAG + 2, name="w")
+            dst = st["w", s][:, tl * CH : (tl + 1) * CH]
+            if bias_on_pe(s, tl):
+                nc.scalar.copy(out=dst, in_=st["pl", s, tl][:])
+            else:
+                nc.vector.tensor_tensor(out=dst, in0=st["pl", s, tl][:], in1=biasb[:], op=ADD)
+
+        def p2(s, tl):
+            dst = st["w", s][:, tl * CH : (tl + 1) * CH]
+            nc.vector.tensor_tensor(out=dst, in0=st["mx", s, tl][:], in1=dst, op=ADD)
+
+        def p3(s, lo, hi):
+            w = st["w", s][:, lo * CH : hi * CH]
+            nc.scalar.activation(out=w, in_=w, func=SIGMOID)
+
+        def p4(s, lo, hi, eng):
+            bh, j = divmod(s, PER_HALF)
+            w3 = st["w", s][:].rearrange("p (t c) -> p t c", t=2)[:, lo:hi, :]
+            c3 = zc[s][:].rearrange("p (t k) -> p t k", t=2)[:, lo:hi, CH:]
+            dst = w3
+            if ACC_MODE == "v" and j == 0:
+                if lo == 0:
+                    st["accp", bh] = work.tile([P, 2 * CH], F32, tag="accp", bufs=2, name="accp")
+                dst = st["accp", bh][:].rearrange("p (t c) -> p t c", t=2)[:, lo:hi, :]
+            eng.tensor_tensor(out=dst, in0=w3, in1=c3, op=MULT)
+
+        def acc_t(s, i):
+            bh, j = divmod(s, PER_HALF)
+            tl, cb = divmod(i, 4)
+            if j == 0 and i == 0:
+                st["acc", bh] = bank("acc", 1)
+            nc.tensor.matmul(
+                out=st["acc", bh][:, cb * P : (cb + 1) * P],
+                lhsT=st["w", s][:, tl * CH + cb * P : tl * CH + (cb + 1) * P],
+                rhs=ident[:],
+                is_transpose=True,
+                start=(j == 0 and i == 0),
+                stop=(j == PER_HALF - 1 and i == 7),
+            )
+
+        def p5(s):
+            bh, j = divmod(s, PER_HALF)
+            if j > 0:
+                a = st["accp", bh]
+                nc.vector.tensor_tensor(out=a[:], in0=a[:], in1=st["w", s][:], op=ADD)
+
+        def store(bh, res):
+            nc.sync.dma_start(out=out[bh * P : (bh + 1) * P, :], in_=res[:])
+
+        def ro_copy(bh):
+            accs = work.tile([P, 512], F32, tag="accs", bufs=1, name="accs")
+            nc.scalar.copy(out=accs[:], in_=st["acc", bh][:])
+            st["accs", bh] = accs
+
+        def ro_back(bh):
+            ops = bank("hps", 1)
+            for cb in range(4):
+                nc.tensor.transpose(
+                    ops[:, cb * P : (cb + 1) * P], st["accs", bh][:, cb * P : (cb + 1) * P], ident[:]
+                )
+            res = work.tile([P, CH], F32, tag="res", bufs=2, name="res")
+            nc.scalar.copy(out=res[:], in_=ops[:])
+            store(bh, res)
+
+        def fin_v(bh):
+            a = st["accp", bh]
+            res = work.tile([P, CH], F32, tag="res", bufs=2, name="res")
+            nc.vector.tensor_tensor(out=res[:], in0=a[:, 0:CH], in1=a[:, CH:], op=ADD)
+            store(bh, res)
+
+        def weave(mats, trans):
+            gaps = len(mats) - 1 if TAIL_FREE else len(mats)
+            done = 0
+            for i, m in enumerate(mats):
+                m()
+                upto = min(len(trans), (len(trans) * (i + 1) + gaps - 1) // gaps)
+                while done < upto:
+                    trans[done]()
+                    done += 1
+            while done < len(trans):
+                trans[done]()
+                done += 1
+
+        ut = const.tile([P, 2 * CH], F32, name="ut")
+        for v in range(2):
+            ups = bank("pl", 2)
+            for t in range(4):
+                nc.tensor.transpose(
+                    ups[:, t * P : (t + 1) * P],
+                    un[:].bitcast(F32)[:, t * 256 + v * P : t * 256 + (v + 1) * P],
+                    ident[:],
+                )
+            if v == 0:
+                nc.scalar.copy(out=ut[:, 0:CH], in_=ups[:])
+            else:
+                nc.vector.tensor_copy(out=ut[:, CH:], in_=ups[:])
+        ut16 = ut[:].bitcast(BF16).rearrange("p (v c e) -> p v c e", v=2, e=2)
+
+        for i in range(4):
+            t_h(0, i)
+        c_h(0)
+
+        bps = bank("acc", 1)
+        nc.tensor.matmul(out=bps[:], lhsT=ones[:], rhs=brow[:], start=True, stop=True)
+        biasb = const.tile([P, CH], F32, name="biasb")
+        nc.vector.tensor_copy(out=biasb[:], in_=bps[:])
+
+        wg = const.tile([P, 2 * CH * 4], BF16, name="wg", align_bytes=64)
+        wg32 = wg[:].bitcast(F32).rearrange("p (g c u) -> p g c u", g=2, u=2)
+        for t in range(4):
+            wps = bank(("zps", "mx")[t % 2], 2)
+            for wb in range(4):
+                nc.tensor.transpose(
+                    wps[:, wb * P : (wb + 1) * P],
+                    wn[:].bitcast(F32)[:, t * 512 + wb * P : t * 512 + (wb + 1) * P],
+                    ident[:],
+                )
+            src = wps[:].rearrange("p (g u c) -> p g c u", g=2, u=2)
+            if t % 2 == 0:
+                nc.scalar.copy(out=wg32[:, :, t * P : (t + 1) * P, :], in_=src)
+            else:
+                nc.vector.tensor_copy(out=wg32[:, :, t * P : (t + 1) * P, :], in_=src)
+        wq = const.tile([P, 2 * CH], U32, name="wq", align_bytes=64)
+        ws = const.tile([P, 2 * CH], U8, name="ws", align_bytes=64)
+        nc.vector.quantize_mx(out=wq[:].bitcast(FP8X4), scales=ws[:], in_=wg[:])
+
+        for s in range(NPAIR + LAG + 2):
+            a = s - LAG
+            m = s - 1
+            mats = []
+            trans = []
+            if s < NPAIR:
+                for tl in range(2):
+                    for i in range(5 if bias_on_pe(s, tl) else 4):
+                        mats.append(lambda s=s, tl=tl, i=i: mm_plain(s, tl, i))
+            if s + 1 < NPAIR:
+                for i in range(4):
+                    trans.append(lambda s=s, i=i: t_h(s + 1, i))
+            if ACC_MODE == "pe" and 0 <= a < NPAIR:
+                for i in range(8):
+                    trans.append(lambda a=a, i=i: acc_t(a, i))
+            if s < NPAIR:
+                for i in range(8):
+                    trans.append(lambda s=s, i=i: t_z(s, i))
+            if ACC_MODE == "v" and 0 <= a < NPAIR:
+                p5(a)
+                if a % PER_HALF == PER_HALF - 1:
+                    fin_v(a // PER_HALF)
+            weave(mats, trans)
+            if s + 1 < NPAIR:
+                c_h(s + 1)
+            if s < NPAIR:
+                c_z(s, 0)
+                c_z(s, 1)
+            if ACC_MODE == "pe":
+                if 0 <= a - 1 < NPAIR and (a - 1) % PER_HALF == PER_HALF - 1:
+                    ro_back((a - 1) // PER_HALF)
+                if 0 <= a < NPAIR and a % PER_HALF == PER_HALF - 1:
+                    ro_copy(a // PER_HALF)
+            if s < NPAIR:
+                p1(s, 0)
+                p1(s, 1)
+            if 0 <= m < NPAIR:
+                for tl in range(2):
+                    for g in range(2):
+                        mm_mx(m, tl, g)
+                if m >= SPLIT_FROM:
+                    for tl in range(2):
+                        p2(m, tl)
+                        p3(m, tl, tl + 1)
+                        p4(m, tl, tl + 1, nc.gpsimd if tl == 0 else nc.vector)
+                else:
+                    p2(m, 0)
+                    p2(m, 1)
+            if s < NPAIR:
+                q_z(s)
+            if 0 <= m < min(NPAIR, SPLIT_FROM):
+                p3(m, 0, 2)
+                p4(m, 0, 2, nc.gpsimd)

@@ -18,11 +18,11 @@ FLOPS = 2 * B * N * (SIZE + CH) * CH
 
 NPAIR = 16
 PER_HALF = 8
-ACC_MODE = "pe"
+ACC_MODE = "pe2"
 LAG = 3
 BIAS_PE = ()
 TAIL_FREE = False
-SPLIT_FROM = 15
+SPLIT_FROM = 14
 
 
 def tile_treelstm_pa_kernel(tc, z_node, z_children, W_f, U_f, b_f, out):
@@ -175,18 +175,25 @@ def tile_treelstm_pa_kernel(tc, z_node, z_children, W_f, U_f, b_f, out):
                 dst = st["accp", bh][:].rearrange("p (t c) -> p t c", t=2)[:, lo:hi, :]
             eng.tensor_tensor(out=dst, in0=w3, in1=c3, op=MULT)
 
-        def acc_t(s, i):
+        def pair_add(s):
+            w = st["w", s]
+            nc.vector.tensor_tensor(out=w[:, 0:CH], in0=w[:, 0:CH], in1=w[:, CH:], op=ADD)
+
+        def summed_tiles(s):
+            return (0,) if (ACC_MODE == "pe2" and s < NPAIR - 1) else (0, 1)
+
+        def acc_t(s, tl, cb):
             bh, j = divmod(s, PER_HALF)
-            tl, cb = divmod(i, 4)
-            if j == 0 and i == 0:
+            first = j == 0 and tl == 0 and cb == 0
+            if first:
                 st["acc", bh] = bank("acc", 1)
             nc.tensor.matmul(
                 out=st["acc", bh][:, cb * P : (cb + 1) * P],
                 lhsT=st["w", s][:, tl * CH + cb * P : tl * CH + (cb + 1) * P],
                 rhs=ident[:],
                 is_transpose=True,
-                start=(j == 0 and i == 0),
-                stop=(j == PER_HALF - 1 and i == 7),
+                start=first,
+                stop=(j == PER_HALF - 1 and tl == summed_tiles(s)[-1] and cb == 3),
             )
 
         def p5(s):
@@ -275,6 +282,12 @@ def tile_treelstm_pa_kernel(tc, z_node, z_children, W_f, U_f, b_f, out):
         ws = const.tile([P, 2 * CH], U8, name="ws", align_bytes=64)
         nc.vector.quantize_mx(out=wq[:].bitcast(FP8X4), scales=ws[:], in_=wg[:])
 
+        on_pe = ACC_MODE in ("pe", "pe2")
+
+        def post(m):
+            p3(m, 0, 2)
+            p4(m, 0, 2, nc.gpsimd)
+
         for s in range(NPAIR + LAG + 2):
             a = s - LAG
             m = s - 1
@@ -287,12 +300,15 @@ def tile_treelstm_pa_kernel(tc, z_node, z_children, W_f, U_f, b_f, out):
             if s + 1 < NPAIR:
                 for i in range(4):
                     trans.append(lambda s=s, i=i: t_h(s + 1, i))
-            if ACC_MODE == "pe" and 0 <= a < NPAIR:
-                for i in range(8):
-                    trans.append(lambda a=a, i=i: acc_t(a, i))
             if s < NPAIR:
                 for i in range(8):
                     trans.append(lambda s=s, i=i: t_z(s, i))
+            if on_pe and 0 <= a < NPAIR:
+                if len(summed_tiles(a)) == 1:
+                    pair_add(a)
+                for tl in summed_tiles(a):
+                    for cb in range(4):
+                        trans.append(lambda a=a, tl=tl, cb=cb: acc_t(a, tl, cb))
             if ACC_MODE == "v" and 0 <= a < NPAIR:
                 p5(a)
                 if a % PER_HALF == PER_HALF - 1:
@@ -300,10 +316,12 @@ def tile_treelstm_pa_kernel(tc, z_node, z_children, W_f, U_f, b_f, out):
             weave(mats, trans)
             if s + 1 < NPAIR:
                 c_h(s + 1)
+            if 0 <= m - 1 < SPLIT_FROM:
+                post(m - 1)
             if s < NPAIR:
                 c_z(s, 0)
                 c_z(s, 1)
-            if ACC_MODE == "pe":
+            if on_pe:
                 if 0 <= a - 1 < NPAIR and (a - 1) % PER_HALF == PER_HALF - 1:
                     ro_back((a - 1) // PER_HALF)
                 if 0 <= a < NPAIR and a % PER_HALF == PER_HALF - 1:
@@ -315,16 +333,12 @@ def tile_treelstm_pa_kernel(tc, z_node, z_children, W_f, U_f, b_f, out):
                 for tl in range(2):
                     for g in range(2):
                         mm_mx(m, tl, g)
-                if m >= SPLIT_FROM:
-                    for tl in range(2):
-                        p2(m, tl)
+                for tl in range(2):
+                    p2(m, tl)
+                    if m >= SPLIT_FROM:
                         p3(m, tl, tl + 1)
-                        p4(m, tl, tl + 1, nc.gpsimd if tl == 0 else nc.vector)
-                else:
-                    p2(m, 0)
-                    p2(m, 1)
             if s < NPAIR:
                 q_z(s)
-            if 0 <= m < min(NPAIR, SPLIT_FROM):
-                p3(m, 0, 2)
-                p4(m, 0, 2, nc.gpsimd)
+            if SPLIT_FROM <= m < NPAIR:
+                p4(m, 0, 1, nc.gpsimd if m < NPAIR - 1 else nc.vector)
+                p4(m, 1, 2, nc.vector)

@@ -18,11 +18,12 @@ FLOPS = 2 * B * N * (SIZE + CH) * CH
 
 NPAIR = 16
 PER_HALF = 8
-ACC_MODE = "pe2"
+ACC_MODE = "pe"
 LAG = 3
 BIAS_PE = ()
 TAIL_FREE = False
-SPLIT_FROM = 14
+P4_ON_V = True
+SPLIT_FROM = 15
 
 
 def tile_treelstm_pa_kernel(tc, z_node, z_children, W_f, U_f, b_f, out):
@@ -283,14 +284,13 @@ def tile_treelstm_pa_kernel(tc, z_node, z_children, W_f, U_f, b_f, out):
         nc.vector.quantize_mx(out=wq[:].bitcast(FP8X4), scales=ws[:], in_=wg[:])
 
         on_pe = ACC_MODE in ("pe", "pe2")
-
-        def post(m):
-            p3(m, 0, 2)
-            p4(m, 0, 2, nc.gpsimd)
+        p4_eng = nc.vector if P4_ON_V else nc.gpsimd
 
         for s in range(NPAIR + LAG + 2):
             a = s - LAG
             m = s - 1
+            f = s - 2
+            whole = 0 <= f < SPLIT_FROM
             mats = []
             trans = []
             if s < NPAIR:
@@ -314,10 +314,10 @@ def tile_treelstm_pa_kernel(tc, z_node, z_children, W_f, U_f, b_f, out):
                 if a % PER_HALF == PER_HALF - 1:
                     fin_v(a // PER_HALF)
             weave(mats, trans)
+            if whole:
+                p3(f, 0, 2)
             if s + 1 < NPAIR:
                 c_h(s + 1)
-            if 0 <= m - 1 < SPLIT_FROM:
-                post(m - 1)
             if s < NPAIR:
                 c_z(s, 0)
                 c_z(s, 1)
@@ -328,6 +328,9 @@ def tile_treelstm_pa_kernel(tc, z_node, z_children, W_f, U_f, b_f, out):
                     ro_copy(a // PER_HALF)
             if s < NPAIR:
                 p1(s, 0)
+            if whole:
+                p4(f, 0, 2, p4_eng)
+            if s < NPAIR:
                 p1(s, 1)
             if 0 <= m < NPAIR:
                 for tl in range(2):
@@ -340,5 +343,5 @@ def tile_treelstm_pa_kernel(tc, z_node, z_children, W_f, U_f, b_f, out):
             if s < NPAIR:
                 q_z(s)
             if SPLIT_FROM <= m < NPAIR:
-                p4(m, 0, 1, nc.gpsimd if m < NPAIR - 1 else nc.vector)
+                p4(m, 0, 1, nc.vector)
                 p4(m, 1, 2, nc.vector)

@@ -21,9 +21,8 @@ PER_HALF = 8
 ACC_MODE = "pe"
 LAG = 3
 BIAS_PE = ()
-TAIL_FREE = False
-P4_ON_V = True
-SPLIT_FROM = 15
+TAIL_FREE = True
+NAT_FROM = NPAIR - 1
 
 
 def tile_treelstm_pa_kernel(tc, z_node, z_children, W_f, U_f, b_f, out):
@@ -59,22 +58,39 @@ def tile_treelstm_pa_kernel(tc, z_node, z_children, W_f, U_f, b_f, out):
             )
             return t
 
+        def load_part(s, lo, nm):
+            bh, j = divmod(s, PER_HALF)
+            t = data.tile([P, 2 * CH], BF16, name="%s%d" % (nm, s))
+            nc.sync.dma_start(
+                out=t[:].rearrange("p (t k) -> p t k", t=2),
+                in_=z_children[bh * P : (bh + 1) * P, 2 * j : 2 * j + 2, lo : lo + CH],
+            )
+            return t[:].rearrange("p (t k) -> p t k", t=2)
+
+        def load_children(s):
+            t = load_pair(z_children, s, "zc")[:].rearrange("p (t k) -> p t k", t=2)
+            hid[s] = t[:, :, 0:CH]
+            cel[s] = t[:, :, CH:]
+
         zn = {}
-        zc = {}
+        hid = {}
+        cel = {}
         un = const.tile([P, 4 * CH], BF16, name="un")
         nc.sync.dma_start(
             out=un[:].rearrange("p (t k) -> p t k", t=4), in_=U_f.rearrange("(t p) k -> p t k", p=P)
         )
-        zc[0] = load_pair(z_children, 0, "zc")
+        hid[0] = load_part(0, 0, "zh")
         wn = const.tile([P, 4 * SIZE], BF16, name="wn")
         nc.sync.dma_start(
             out=wn[:].rearrange("p (t k) -> p t k", t=4), in_=W_f.rearrange("(t p) k -> p t k", p=P)
         )
-        zc[1] = load_pair(z_children, 1, "zc")
         zn[0] = load_pair(z_node, 0, "zn")
+        hid[1] = load_part(1, 0, "zh")
+        cel[0] = load_part(0, CH, "zcc")
+        cel[1] = load_part(1, CH, "zcc")
         for s in range(1, NPAIR):
             if s + 1 < NPAIR:
-                zc[s + 1] = load_pair(z_children, s + 1, "zc")
+                load_children(s + 1)
             zn[s] = load_pair(z_node, s, "zn")
 
         def t_h(s, i):
@@ -83,7 +99,7 @@ def tile_treelstm_pa_kernel(tc, z_node, z_children, W_f, U_f, b_f, out):
             tl, v = divmod(i, 2)
             nc.tensor.transpose(
                 st["hps", s][:, i * P : (i + 1) * P],
-                zc[s][:].bitcast(F32)[:, tl * 512 + v * P : tl * 512 + (v + 1) * P],
+                hid[s][:, tl, :].bitcast(F32)[:, v * P : (v + 1) * P],
                 ident[:],
             )
 
@@ -168,7 +184,7 @@ def tile_treelstm_pa_kernel(tc, z_node, z_children, W_f, U_f, b_f, out):
         def p4(s, lo, hi, eng):
             bh, j = divmod(s, PER_HALF)
             w3 = st["w", s][:].rearrange("p (t c) -> p t c", t=2)[:, lo:hi, :]
-            c3 = zc[s][:].rearrange("p (t k) -> p t k", t=2)[:, lo:hi, CH:]
+            c3 = cel[s][:, lo:hi, :]
             dst = w3
             if ACC_MODE == "v" and j == 0:
                 if lo == 0:
@@ -194,7 +210,7 @@ def tile_treelstm_pa_kernel(tc, z_node, z_children, W_f, U_f, b_f, out):
                 rhs=ident[:],
                 is_transpose=True,
                 start=first,
-                stop=(j == PER_HALF - 1 and tl == summed_tiles(s)[-1] and cb == 3),
+                stop=((j == PER_HALF - 1 or s == NAT_FROM - 1) and tl == 1 and cb == 3),
             )
 
         def p5(s):
@@ -211,15 +227,17 @@ def tile_treelstm_pa_kernel(tc, z_node, z_children, W_f, U_f, b_f, out):
             nc.scalar.copy(out=accs[:], in_=st["acc", bh][:])
             st["accs", bh] = accs
 
-        def ro_back(bh):
+        def ro_back(bh, finish):
             ops = bank("hps", 1)
+            st["ops", bh] = ops
             for cb in range(4):
                 nc.tensor.transpose(
                     ops[:, cb * P : (cb + 1) * P], st["accs", bh][:, cb * P : (cb + 1) * P], ident[:]
                 )
-            res = work.tile([P, CH], F32, tag="res", bufs=2, name="res")
-            nc.scalar.copy(out=res[:], in_=ops[:])
-            store(bh, res)
+            if finish:
+                res = work.tile([P, CH], F32, tag="res", bufs=2, name="res")
+                nc.scalar.copy(out=res[:], in_=ops[:])
+                store(bh, res)
 
         def fin_v(bh):
             a = st["accp", bh]
@@ -265,83 +283,100 @@ def tile_treelstm_pa_kernel(tc, z_node, z_children, W_f, U_f, b_f, out):
         nc.vector.tensor_copy(out=biasb[:], in_=bps[:])
 
         wg = const.tile([P, 2 * CH * 4], BF16, name="wg", align_bytes=64)
-        wg32 = wg[:].bitcast(F32).rearrange("p (g c u) -> p g c u", g=2, u=2)
-        for t in range(4):
-            wps = bank(("zps", "mx")[t % 2], 2)
-            for wb in range(4):
-                nc.tensor.transpose(
-                    wps[:, wb * P : (wb + 1) * P],
-                    wn[:].bitcast(F32)[:, t * 512 + wb * P : t * 512 + (wb + 1) * P],
-                    ident[:],
-                )
-            src = wps[:].rearrange("p (g u c) -> p g c u", g=2, u=2)
-            if t % 2 == 0:
-                nc.scalar.copy(out=wg32[:, :, t * P : (t + 1) * P, :], in_=src)
-            else:
-                nc.vector.tensor_copy(out=wg32[:, :, t * P : (t + 1) * P, :], in_=src)
         wq = const.tile([P, 2 * CH], U32, name="wq", align_bytes=64)
         ws = const.tile([P, 2 * CH], U8, name="ws", align_bytes=64)
-        nc.vector.quantize_mx(out=wq[:].bitcast(FP8X4), scales=ws[:], in_=wg[:])
 
-        on_pe = ACC_MODE in ("pe", "pe2")
-        p4_eng = nc.vector if P4_ON_V else nc.gpsimd
+        def t_w(i):
+            q, r = divmod(i, 4)
+            g, hh = divmod(q, 2)
+            u, t = divmod(r, 2)
+            if r == 0:
+                st["wps", q] = bank(("zps", "mx")[q % 2], 2)
+            nc.tensor.transpose(
+                st["wps", q][:, r * P : (r + 1) * P],
+                wn[:].bitcast(F32)[:, (2 * hh + t) * 512 + (2 * g + u) * P : (2 * hh + t) * 512 + (2 * g + u + 1) * P],
+                ident[:],
+            )
 
-        for s in range(NPAIR + LAG + 2):
+        def c_w():
+            for q in range(4):
+                src = st["wps", q][:].rearrange("p (u x) -> p x u", u=2)
+                dst = wg[:].bitcast(F32)[:, q * 512 : (q + 1) * 512].rearrange("p (x u) -> p x u", u=2)
+                if q % 2 == 0:
+                    nc.scalar.copy(out=dst, in_=src)
+                else:
+                    nc.vector.tensor_copy(out=dst, in_=src)
+            nc.vector.quantize_mx(out=wq[:].bitcast(FP8X4), scales=ws[:], in_=wg[:])
+
+        def half(s, tl):
+            return st["w", s][:, tl * CH : (tl + 1) * CH]
+
+        def add_v(dst, x, y):
+            nc.vector.tensor_tensor(out=dst, in0=x, in1=y, op=ADD)
+
+        LAST = NPAIR - 1
+        for s in range(NPAIR):
             a = s - LAG
             m = s - 1
-            f = s - 2
-            whole = 0 <= f < SPLIT_FROM
             mats = []
-            trans = []
-            if s < NPAIR:
-                for tl in range(2):
-                    for i in range(5 if bias_on_pe(s, tl) else 4):
-                        mats.append(lambda s=s, tl=tl, i=i: mm_plain(s, tl, i))
-            if s + 1 < NPAIR:
-                for i in range(4):
-                    trans.append(lambda s=s, i=i: t_h(s + 1, i))
-            if s < NPAIR:
-                for i in range(8):
-                    trans.append(lambda s=s, i=i: t_z(s, i))
-            if on_pe and 0 <= a < NPAIR:
-                if len(summed_tiles(a)) == 1:
-                    pair_add(a)
-                for tl in summed_tiles(a):
-                    for cb in range(4):
-                        trans.append(lambda a=a, tl=tl, cb=cb: acc_t(a, tl, cb))
-            if ACC_MODE == "v" and 0 <= a < NPAIR:
-                p5(a)
-                if a % PER_HALF == PER_HALF - 1:
-                    fin_v(a // PER_HALF)
-            weave(mats, trans)
-            if whole:
-                p3(f, 0, 2)
-            if s + 1 < NPAIR:
+            for tl in range(2):
+                for i in range(5 if bias_on_pe(s, tl) else 4):
+                    mats.append(lambda s=s, tl=tl, i=i: mm_plain(s, tl, i))
+            t_hs = [lambda s=s, i=i: t_h(s + 1, i) for i in range(4)] if s < LAST else []
+            t_zs = [lambda s=s, i=i: t_z(s, i) for i in range(8)]
+            accs = [lambda a=a, i=i: acc_t(a, i // 4, i % 4) for i in range(8)] if a >= 0 else []
+            if s == 0:
+                weave(mats[:4], [lambda i=i: t_w(i) for i in range(16)])
+                p1(0, 0)
+                c_w()
+                mats = mats[4:]
+            weave(mats, t_zs + accs if s == LAST else t_hs + accs + t_zs)
+            if s < LAST:
                 c_h(s + 1)
-            if s < NPAIR:
-                c_z(s, 0)
-                c_z(s, 1)
-            if on_pe:
-                if 0 <= a - 1 < NPAIR and (a - 1) % PER_HALF == PER_HALF - 1:
-                    ro_back((a - 1) // PER_HALF)
-                if 0 <= a < NPAIR and a % PER_HALF == PER_HALF - 1:
-                    ro_copy(a // PER_HALF)
-            if s < NPAIR:
+            c_z(s, 0)
+            c_z(s, 1)
+            if a == PER_HALF:
+                ro_back(0, True)
+            if a == PER_HALF - 1:
+                ro_copy(0)
+            if s > 0:
                 p1(s, 0)
-            if whole:
-                p4(f, 0, 2, p4_eng)
-            if s < NPAIR:
-                p1(s, 1)
-            if 0 <= m < NPAIR:
+            if s == LAST:
+                q_z(s)
+            p1(s, 1)
+            if m >= 0:
                 for tl in range(2):
                     for g in range(2):
                         mm_mx(m, tl, g)
-                for tl in range(2):
-                    p2(m, tl)
-                    if m >= SPLIT_FROM:
-                        p3(m, tl, tl + 1)
-            if s < NPAIR:
+            if s < LAST:
+                if m >= 0:
+                    p2(m, 0)
+                    p2(m, 1)
                 q_z(s)
-            if SPLIT_FROM <= m < NPAIR:
-                p4(m, 0, 1, nc.vector)
-                p4(m, 1, 2, nc.vector)
+                if m >= 0:
+                    p3(m, 0, 2)
+                    p4(m, 0, 2, nc.gpsimd)
+
+        p2(LAST - 1, 0)
+        p3(LAST - 1, 0, 1)
+        p4(LAST - 1, 0, 1, nc.gpsimd)
+        p2(LAST - 1, 1)
+        p3(LAST - 1, 1, 2)
+        for tl in range(2):
+            for g in range(2):
+                mm_mx(LAST, tl, g)
+        for tl in range(2):
+            p2(LAST, tl)
+            p3(LAST, tl, tl + 1)
+        p4(LAST - 1, 1, 2, nc.vector)
+        for a in (LAST - 2, LAST - 1):
+            for i in range(8):
+                acc_t(a, i // 4, i % 4)
+        ro_copy(1)
+        ro_back(1, False)
+        p4(LAST, 0, 1, nc.vector)
+        p4(LAST, 1, 2, nc.vector)
+        add_v(half(LAST, 0), half(LAST, 0), half(LAST, 1))
+        res = work.tile([P, CH], F32, tag="res", bufs=2, name="res")
+        add_v(res[:], st["ops", 1][:], half(LAST, 0))
+        store(1, res)

@@ -18,7 +18,7 @@ FLOPS = 2 * B * N * (SIZE + CH) * CH
 
 NPAIR = 16
 PER_HALF = 8
-ACC_MODE = "pe"
+ACC_MODE = "g"
 LAG = 3
 BIAS_PE = ()
 TAIL_FREE = True
@@ -95,7 +95,7 @@ def tile_treelstm_pa_kernel(tc, z_node, z_children, W_f, U_f, b_f, out):
 
         def t_h(s, i):
             if i == 0:
-                st["hps", s] = bank("hps", 1)
+                st["hps", s] = bank("hps", 2)
             tl, v = divmod(i, 2)
             nc.tensor.transpose(
                 st["hps", s][:, i * P : (i + 1) * P],
@@ -228,7 +228,7 @@ def tile_treelstm_pa_kernel(tc, z_node, z_children, W_f, U_f, b_f, out):
             st["accs", bh] = accs
 
         def ro_back(bh, finish):
-            ops = bank("hps", 1)
+            ops = bank("hps", 2)
             st["ops", bh] = ops
             for cb in range(4):
                 nc.tensor.transpose(
@@ -277,7 +277,7 @@ def tile_treelstm_pa_kernel(tc, z_node, z_children, W_f, U_f, b_f, out):
             t_h(0, i)
         c_h(0)
 
-        bps = bank("acc", 1)
+        bps = bank("hps", 2)
         nc.tensor.matmul(out=bps[:], lhsT=ones[:], rhs=brow[:], start=True, stop=True)
         biasb = const.tile([P, CH], F32, name="biasb")
         nc.vector.tensor_copy(out=biasb[:], in_=bps[:])
@@ -315,35 +315,53 @@ def tile_treelstm_pa_kernel(tc, z_node, z_children, W_f, U_f, b_f, out):
             nc.vector.tensor_tensor(out=dst, in0=x, in1=y, op=ADD)
 
         LAST = NPAIR - 1
+
+        def p4v(s, lo, hi):
+            bh, j = divmod(s, PER_HALF)
+            w3 = st["w", s][:].rearrange("p (t c) -> p t c", t=2)[:, lo:hi, :]
+            dst = w3
+            if j == 0:
+                st["accp", bh] = work.tile([P, 2 * CH], F32, tag="accp", bufs=2, name="accp")
+                dst = st["accp", bh][:].rearrange("p (t c) -> p t c", t=2)
+            nc.vector.tensor_tensor(out=dst, in0=w3, in1=cel[s][:, lo:hi, :], op=MULT)
+
+        def p5g(s):
+            bh, j = divmod(s, PER_HALF)
+            acc = st["accp", bh]
+            if j > 0:
+                nc.gpsimd.tensor_tensor(out=acc[:], in0=acc[:], in1=st["w", s][:], op=ADD)
+            if s == PER_HALF - 1:
+                res = work.tile([P, CH], F32, tag="res", bufs=2, name="res")
+                nc.gpsimd.tensor_tensor(out=res[:], in0=acc[:, 0:CH], in1=acc[:, CH:], op=ADD)
+                store(0, res)
+
         for s in range(NPAIR):
-            a = s - LAG
             m = s - 1
+            f = s - 2
             mats = []
             for tl in range(2):
                 for i in range(5 if bias_on_pe(s, tl) else 4):
                     mats.append(lambda s=s, tl=tl, i=i: mm_plain(s, tl, i))
             t_hs = [lambda s=s, i=i: t_h(s + 1, i) for i in range(4)] if s < LAST else []
             t_zs = [lambda s=s, i=i: t_z(s, i) for i in range(8)]
-            accs = [lambda a=a, i=i: acc_t(a, i // 4, i % 4) for i in range(8)] if a >= 0 else []
             if s == 0:
                 weave(mats[:4], [lambda i=i: t_w(i) for i in range(16)])
                 p1(0, 0)
                 c_w()
                 mats = mats[4:]
-            weave(mats, t_zs + accs if s == LAST else t_hs + accs + t_zs)
+            weave(mats, t_hs + t_zs)
             if s < LAST:
                 c_h(s + 1)
             c_z(s, 0)
             c_z(s, 1)
-            if a == PER_HALF:
-                ro_back(0, True)
-            if a == PER_HALF - 1:
-                ro_copy(0)
             if s > 0:
                 p1(s, 0)
             if s == LAST:
+                p4v(f, 0, 2)
+                p5g(f)
                 q_z(s)
-            p1(s, 1)
+            else:
+                p1(s, 1)
             if m >= 0:
                 for tl in range(2):
                     for g in range(2):
@@ -355,28 +373,30 @@ def tile_treelstm_pa_kernel(tc, z_node, z_children, W_f, U_f, b_f, out):
                 q_z(s)
                 if m >= 0:
                     p3(m, 0, 2)
-                    p4(m, 0, 2, nc.gpsimd)
+                if f >= 0:
+                    p4v(f, 0, 2)
+                    p5g(f)
 
         p2(LAST - 1, 0)
         p3(LAST - 1, 0, 1)
-        p4(LAST - 1, 0, 1, nc.gpsimd)
         p2(LAST - 1, 1)
         p3(LAST - 1, 1, 2)
+        p1(LAST, 1)
         for tl in range(2):
             for g in range(2):
                 mm_mx(LAST, tl, g)
+        tot = half(LAST - 1, 0)
+        acc = st["accp", 1]
+        nc.gpsimd.tensor_tensor(out=acc[:, 0:CH], in0=acc[:, 0:CH], in1=acc[:, CH:], op=ADD)
         for tl in range(2):
             p2(LAST, tl)
             p3(LAST, tl, tl + 1)
-        p4(LAST - 1, 1, 2, nc.vector)
-        for a in (LAST - 2, LAST - 1):
-            for i in range(8):
-                acc_t(a, i // 4, i % 4)
-        ro_copy(1)
-        ro_back(1, False)
-        p4(LAST, 0, 1, nc.vector)
-        p4(LAST, 1, 2, nc.vector)
-        add_v(half(LAST, 0), half(LAST, 0), half(LAST, 1))
+        p4v(LAST - 1, 0, 2)
+        add_v(tot, tot, half(LAST - 1, 1))
+        p4v(LAST, 0, 1)
+        add_v(tot, tot, half(LAST, 0))
+        add_v(tot, tot, acc[:, 0:CH])
+        p4v(LAST, 1, 2)
         res = work.tile([P, CH], F32, tag="res", bufs=2, name="res")
-        add_v(res[:], st["ops", 1][:], half(LAST, 0))
+        add_v(res[:], tot, half(LAST, 1))
         store(1, res)

@@ -20,7 +20,7 @@ NPAIR = 16
 PER_HALF = 8
 ACC_MODE = "g"
 LAG = 3
-BIAS_PE = ()
+BIAS_PE = (1, 3, 5, 7)
 TAIL_FREE = True
 NAT_FROM = NPAIR - 1
 
@@ -134,7 +134,7 @@ def tile_treelstm_pa_kernel(tc, z_node, z_children, W_f, U_f, b_f, out):
             st["zq", s] = (zq, zs)
 
         def bias_on_pe(s, tl):
-            return (2 * s + tl) % 8 in BIAS_PE
+            return (2 * s + tl) % 8 in BIAS_PE or s >= NPAIR - 2
 
         def mm_plain(s, tl, i):
             if i == 0:

from contextlib import ExitStack

import concourse.mybir as mybir
from concourse.masks import make_identity

F32 = mybir.dt.float32
BF16 = mybir.dt.bfloat16
U32 = mybir.dt.uint32
U8 = mybir.dt.uint8
FP8X4 = mybir.dt.float8_e4m3fn_x4
ADD = mybir.AluOpType.add
MULT = mybir.AluOpType.mult
SIGMOID = mybir.ActivationFunctionType.Sigmoid

P = 128
B, N, SIZE, CH = 256, 16, 1024, 512
FLOPS = 2 * B * N * (SIZE + CH) * CH

NPAIR = 16
PER_HALF = 8
ACC_MODE = "g"
LAG = 3
BIAS_PE = (1, 3, 5, 7)
TAIL_FREE = True
NAT_FROM = NPAIR - 1


def tile_treelstm_pa_kernel(tc, z_node, z_children, W_f, U_f, b_f, out):
    nc = tc.nc
    st = {}
    with ExitStack() as ctx:
        const = ctx.enter_context(tc.tile_pool(name="const", bufs=1))
        data = ctx.enter_context(tc.tile_pool(name="data", bufs=1))
        work = ctx.enter_context(tc.tile_pool(name="work", bufs=2))
        psum = ctx.enter_context(tc.psum_pool(name="psum", bufs=1))
        ctx.enter_context(tc.manual_schedule())

        def bank(tag, bufs):
            return psum.tile([P, 512], F32, tag=tag, bufs=bufs, name=tag)

        brow = const.tile([P, CH], BF16, name="brow")
        nc.vector.memset(brow[:], 0.0)
        nc.scalar.dma_start(out=brow[0:1, :], in_=b_f.rearrange("(o c) -> o c", o=1))
        ones = const.tile([P, P], BF16, name="ones")
        nc.vector.memset(ones[:], 1.0)
        warm = const.tile([P, 8], F32, name="warm")
        nc.vector.memset(warm[:], 0.0)
        nc.scalar.activation(out=warm[:], in_=warm[:], func=SIGMOID)
        ident = const.tile([P, P], F32, name="ident")
        make_identity(nc, ident[:])

        def load_pair(src, s, nm):
            bh, j = divmod(s, PER_HALF)
            t = data.tile([P, 2 * SIZE], BF16, name="%s%d" % (nm, s))
            nc.sync.dma_start(
                out=t[:],
                in_=src[bh * P : (bh + 1) * P, 2 * j : 2 * j + 2, :].rearrange("b n k -> b (n k)"),
            )
            return t

        def load_part(s, lo, nm):
            bh, j = divmod(s, PER_HALF)
            t = data.tile([P, 2 * CH], BF16, name="%s%d" % (nm, s))
            nc.sync.dma_start(
                out=t[:].rearrange("p (t k) -> p t k", t=2),
                in_=z_children[bh * P : (bh + 1) * P, 2 * j : 2 * j + 2, lo : lo + CH],
            )
            return t[:].rearrange("p (t k) -> p t k", t=2)

        def load_children(s):
            t = load_pair(z_children, s, "zc")[:].rearrange("p (t k) -> p t k", t=2)
            hid[s] = t[:, :, 0:CH]
            cel[s] = t[:, :, CH:]

        zn = {}
        hid = {}
        cel = {}
        un = const.tile([P, 4 * CH], BF16, name="un")
        nc.sync.dma_start(
            out=un[:].rearrange("p (t k) -> p t k", t=4), in_=U_f.rearrange("(t p) k -> p t k", p=P)
        )
        hid[0] = load_part(0, 0, "zh")
        wn = const.tile([P, 4 * SIZE], BF16, name="wn")
        nc.sync.dma_start(
            out=wn[:].rearrange("p (t k) -> p t k", t=4), in_=W_f.rearrange("(t p) k -> p t k", p=P)
        )
        zn[0] = load_pair(z_node, 0, "zn")
        hid[1] = load_part(1, 0, "zh")
        cel[0] = load_part(0, CH, "zcc")
        cel[1] = load_part(1, CH, "zcc")
        for s in range(1, NPAIR):
            if s + 1 < NPAIR:
                load_children(s + 1)
            zn[s] = load_pair(z_node, s, "zn")

        def t_h(s, i):
            if i == 0:
                st["hps", s] = bank("hps", 2)
            tl, v = divmod(i, 2)
            nc.tensor.transpose(
                st["hps", s][:, i * P : (i + 1) * P],
                hid[s][:, tl, :].bitcast(F32)[:, v * P : (v + 1) * P],
                ident[:],
            )

        def c_h(s):
            ht = work.tile([P, 512], F32, tag="ht", bufs=2, name="ht")
            nc.scalar.copy(out=ht[:], in_=st["hps", s][:])
            st["ht", s] = ht[:].bitcast(BF16).rearrange("p (t v r e) -> p t v r e", t=2, v=2, e=2)

        def t_z(s, i):
            tl, wb = divmod(i, 4)
            if wb == 0:
                st["zps", s, tl] = bank("zps", 2)
            nc.tensor.transpose(
                st["zps", s, tl][:, wb * P : (wb + 1) * P],
                zn[s][:].bitcast(F32)[:, tl * 512 + wb * P : tl * 512 + (wb + 1) * P],
                ident[:],
            )

        def c_z(s, tl):
            if tl == 0:
                st["zg", s] = work.tile([P, 2048], BF16, tag="zg", bufs=2, name="zg", align_bytes=64)
            dst = st["zg", s][:].bitcast(F32)[:, tl * 512 : (tl + 1) * 512]
            nc.scalar.copy(
                out=dst.rearrange("p (g r u) -> p g r u", g=2, u=2),
                in_=st["zps", s, tl][:].rearrange("p (g u r) -> p g r u", g=2, u=2),
            )

        def q_z(s):
            zq = work.tile([P, 512], U32, tag="zq", bufs=3, name="zq", align_bytes=64)
            zs = work.tile([P, 512], U8, tag="zs", bufs=3, name="zs", align_bytes=64)
            nc.vector.quantize_mx(out=zq[:].bitcast(FP8X4), scales=zs[:], in_=st["zg", s][:])
            st["zq", s] = (zq, zs)

        def bias_on_pe(s, tl):
            return (2 * s + tl) % 8 in BIAS_PE or s >= NPAIR - 2

        def mm_plain(s, tl, i):
            if i == 0:
                st["pl", s, tl] = bank("pl", 2)
            last = 4 if bias_on_pe(s, tl) else 3
            if i < 4:
                v, e = divmod(i, 2)
                lhs = st["ht", s][:, tl, v, :, e]
                rhs = ut16[:, v, :, e]
            else:
                lhs = ones[:]
                rhs = brow[:]
            nc.tensor.matmul(out=st["pl", s, tl][:], lhsT=lhs, rhs=rhs, start=(i == 0), stop=(i == last))

        def mm_mx(s, tl, g):
            if g == 0:
                st["mx", s, tl] = bank("mx", 2)
            zq, zs = st["zq", s]
            c0 = (tl * 2 + g) * P
            nc.tensor.matmul_mx(
                out=st["mx", s, tl][:],
                lhsT=zq[:, c0 : c0 + P].bitcast(FP8X4),
                lhsT_scale=zs[:, c0 : c0 + P],
                rhs=wq[:, g * CH : (g + 1) * CH].bitcast(FP8X4),
                rhs_scale=ws[:, g * CH : (g + 1) * CH],
                start=(g == 0),
                stop=(g == 1),
            )

        def p1(s, tl):
            if tl == 0:
                st["w", s] = work.tile([P, 2 * CH], F32, tag="w", bufs=LAG + 2, name="w")
            dst = st["w", s][:, tl * CH : (tl + 1) * CH]
            if bias_on_pe(s, tl):
                nc.scalar.copy(out=dst, in_=st["pl", s, tl][:])
            else:
                nc.vector.tensor_tensor(out=dst, in0=st["pl", s, tl][:], in1=biasb[:], op=ADD)

        def p2(s, tl):
            dst = st["w", s][:, tl * CH : (tl + 1) * CH]
            nc.vector.tensor_tensor(out=dst, in0=st["mx", s, tl][:], in1=dst, op=ADD)

        def p3(s, lo, hi):
            w = st["w", s][:, lo * CH : hi * CH]
            nc.scalar.activation(out=w, in_=w, func=SIGMOID)

        def p4(s, lo, hi, eng):
            bh, j = divmod(s, PER_HALF)
            w3 = st["w", s][:].rearrange("p (t c) -> p t c", t=2)[:, lo:hi, :]
            c3 = cel[s][:, lo:hi, :]
            dst = w3
            if ACC_MODE == "v" and j == 0:
                if lo == 0:
                    st["accp", bh] = work.tile([P, 2 * CH], F32, tag="accp", bufs=2, name="accp")
                dst = st["accp", bh][:].rearrange("p (t c) -> p t c", t=2)[:, lo:hi, :]
            eng.tensor_tensor(out=dst, in0=w3, in1=c3, op=MULT)

        def pair_add(s):
            w = st["w", s]
            nc.vector.tensor_tensor(out=w[:, 0:CH], in0=w[:, 0:CH], in1=w[:, CH:], op=ADD)

        def summed_tiles(s):
            return (0,) if (ACC_MODE == "pe2" and s < NPAIR - 1) else (0, 1)

        def acc_t(s, tl, cb):
            bh, j = divmod(s, PER_HALF)
            first = j == 0 and tl == 0 and cb == 0
            if first:
                st["acc", bh] = bank("acc", 1)
            nc.tensor.matmul(
                out=st["acc", bh][:, cb * P : (cb + 1) * P],
                lhsT=st["w", s][:, tl * CH + cb * P : tl * CH + (cb + 1) * P],
                rhs=ident[:],
                is_transpose=True,
                start=first,
                stop=((j == PER_HALF - 1 or s == NAT_FROM - 1) and tl == 1 and cb == 3),
            )

        def p5(s):
            bh, j = divmod(s, PER_HALF)
            if j > 0:
                a = st["accp", bh]
                nc.vector.tensor_tensor(out=a[:], in0=a[:], in1=st["w", s][:], op=ADD)

        def store(bh, res):
            nc.sync.dma_start(out=out[bh * P : (bh + 1) * P, :], in_=res[:])

        def ro_copy(bh):
            accs = work.tile([P, 512], F32, tag="accs", bufs=1, name="accs")
            nc.scalar.copy(out=accs[:], in_=st["acc", bh][:])
            st["accs", bh] = accs

        def ro_back(bh, finish):
            ops = bank("hps", 2)
            st["ops", bh] = ops
            for cb in range(4):
                nc.tensor.transpose(
                    ops[:, cb * P : (cb + 1) * P], st["accs", bh][:, cb * P : (cb + 1) * P], ident[:]
                )
            if finish:
                res = work.tile([P, CH], F32, tag="res", bufs=2, name="res")
                nc.scalar.copy(out=res[:], in_=ops[:])
                store(bh, res)

        def fin_v(bh):
            a = st["accp", bh]
            res = work.tile([P, CH], F32, tag="res", bufs=2, name="res")
            nc.vector.tensor_tensor(out=res[:], in0=a[:, 0:CH], in1=a[:, CH:], op=ADD)
            store(bh, res)

        def weave(mats, trans):
            gaps = len(mats) - 1 if TAIL_FREE else len(mats)
            done = 0
            for i, m in enumerate(mats):
                m()
                upto = min(len(trans), (len(trans) * (i + 1) + gaps - 1) // gaps)
                while done < upto:
                    trans[done]()
                    done += 1
            while done < len(trans):
                trans[done]()
                done += 1

        ut = const.tile([P, 2 * CH], F32, name="ut")
        for v in range(2):
            ups = bank("pl", 2)
            for t in range(4):
                nc.tensor.transpose(
                    ups[:, t * P : (t + 1) * P],
                    un[:].bitcast(F32)[:, t * 256 + v * P : t * 256 + (v + 1) * P],
                    ident[:],
                )
            if v == 0:
                nc.scalar.copy(out=ut[:, 0:CH], in_=ups[:])
            else:
                nc.vector.tensor_copy(out=ut[:, CH:], in_=ups[:])
        ut16 = ut[:].bitcast(BF16).rearrange("p (v c e) -> p v c e", v=2, e=2)

        for i in range(4):
            t_h(0, i)
        c_h(0)

        bps = bank("hps", 2)
        nc.tensor.matmul(out=bps[:], lhsT=ones[:], rhs=brow[:], start=True, stop=True)
        biasb = const.tile([P, CH], F32, name="biasb")
        nc.vector.tensor_copy(out=biasb[:], in_=bps[:])

        wg = const.tile([P, 2 * CH * 4], BF16, name="wg", align_bytes=64)
        wq = const.tile([P, 2 * CH], U32, name="wq", align_bytes=64)
        ws = const.tile([P, 2 * CH], U8, name="ws", align_bytes=64)

        def t_w(i):
            q, r = divmod(i, 4)
            g, hh = divmod(q, 2)
            u, t = divmod(r, 2)
            if r == 0:
                st["wps", q] = bank(("zps", "mx")[q % 2], 2)
            nc.tensor.transpose(
                st["wps", q][:, r * P : (r + 1) * P],
                wn[:].bitcast(F32)[:, (2 * hh + t) * 512 + (2 * g + u) * P : (2 * hh + t) * 512 + (2 * g + u + 1) * P],
                ident[:],
            )

        def c_w():
            for q in range(4):
                src = st["wps", q][:].rearrange("p (u x) -> p x u", u=2)
                dst = wg[:].bitcast(F32)[:, q * 512 : (q + 1) * 512].rearrange("p (x u) -> p x u", u=2)
                if q % 2 == 0:
                    nc.scalar.copy(out=dst, in_=src)
                else:
                    nc.vector.tensor_copy(out=dst, in_=src)
            nc.vector.quantize_mx(out=wq[:].bitcast(FP8X4), scales=ws[:], in_=wg[:])

        def half(s, tl):
            return st["w", s][:, tl * CH : (tl + 1) * CH]

        def add_v(dst, x, y):
            nc.vector.tensor_tensor(out=dst, in0=x, in1=y, op=ADD)

        LAST = NPAIR - 1

        def p4v(s, lo, hi):
            bh, j = divmod(s, PER_HALF)
            w3 = st["w", s][:].rearrange("p (t c) -> p t c", t=2)[:, lo:hi, :]
            dst = w3
            if j == 0:
                st["accp", bh] = work.tile([P, 2 * CH], F32, tag="accp", bufs=2, name="accp")
                dst = st["accp", bh][:].rearrange("p (t c) -> p t c", t=2)
            nc.vector.tensor_tensor(out=dst, in0=w3, in1=cel[s][:, lo:hi, :], op=MULT)

        def p5g(s):
            bh, j = divmod(s, PER_HALF)
            acc = st["accp", bh]
            if j > 0:
                nc.gpsimd.tensor_tensor(out=acc[:], in0=acc[:], in1=st["w", s][:], op=ADD)
            if s == PER_HALF - 1:
                res = work.tile([P, CH], F32, tag="res", bufs=2, name="res")
                nc.gpsimd.tensor_tensor(out=res[:], in0=acc[:, 0:CH], in1=acc[:, CH:], op=ADD)
                store(0, res)

        for s in range(NPAIR):
            m = s - 1
            f = s - 2
            mats = []
            for tl in range(2):
                for i in range(5 if bias_on_pe(s, tl) else 4):
                    mats.append(lambda s=s, tl=tl, i=i: mm_plain(s, tl, i))
            t_hs = [lambda s=s, i=i: t_h(s + 1, i) for i in range(4)] if s < LAST else []
            t_zs = [lambda s=s, i=i: t_z(s, i) for i in range(8)]
            if s == 0:
                weave(mats[:4], [lambda i=i: t_w(i) for i in range(16)])
                p1(0, 0)
                c_w()
                mats = mats[4:]
            weave(mats, t_hs + t_zs)
            if s < LAST:
                c_h(s + 1)
            c_z(s, 0)
            c_z(s, 1)
            if s > 0:
                p1(s, 0)
            if s == LAST:
                p4v(f, 0, 2)
                p5g(f)
                q_z(s)
            else:
                p1(s, 1)
            if m >= 0:
                for tl in range(2):
                    for g in range(2):
                        mm_mx(m, tl, g)
            if s < LAST:
                if m >= 0:
                    p2(m, 0)
                    p2(m, 1)
                q_z(s)
                if m >= 0:
                    p3(m, 0, 2)
                if f >= 0:
                    p4v(f, 0, 2)
                    p5g(f)

        p2(LAST - 1, 0)
        p3(LAST - 1, 0, 1)
        p2(LAST - 1, 1)
        p3(LAST - 1, 1, 2)
        p1(LAST, 1)
        for tl in range(2):
            for g in range(2):
                mm_mx(LAST, tl, g)
        tot = half(LAST - 1, 0)
        acc = st["accp", 1]
        nc.gpsimd.tensor_tensor(out=acc[:, 0:CH], in0=acc[:, 0:CH], in1=acc[:, CH:], op=ADD)
        for tl in range(2):
            p2(LAST, tl)
            p3(LAST, tl, tl + 1)
        p4v(LAST - 1, 0, 2)
        add_v(tot, tot, half(LAST - 1, 1))
        p4v(LAST, 0, 1)
        add_v(tot, tot, half(LAST, 0))
        add_v(tot, tot, acc[:, 0:CH])
        p4v(LAST, 1, 2)
        res = work.tile([P, CH], F32, tag="res", bufs=2, name="res")
        add_v(res[:], tot, half(LAST, 1))
        store(1, res)
